import numpy as np
import ml_dtypes


def mxq(x, axis, fmt="e4m3"):
    dtype, down = {"e4m3": (ml_dtypes.float8_e4m3fn, 7), "e5m2": (ml_dtypes.float8_e5m2, 14)}[fmt]
    v = np.moveaxis(np.asarray(x, np.float32).astype(ml_dtypes.bfloat16).astype(np.float64), axis, -1)
    blocks = v.reshape(v.shape[:-1] + (-1, 32))
    amax = np.abs(blocks).max(-1, keepdims=True)
    byte = np.maximum(np.where(amax > 0, np.frexp(amax)[1] - 1 + 127, 0) - down, 1)
    scale = np.exp2(byte - 127.0)
    codes = (blocks / scale).astype(np.float32).astype(dtype).astype(np.float64)
    return np.moveaxis((codes * scale).reshape(v.shape), -1, axis)


WIDE = False


def mx_kscale(k):
    if not WIDE:
        return np.ones(k)
    levels = np.array([10, -10, 5, -5, 0])
    a = np.random.permutation(np.resize(levels, k // 512 * 4)).reshape(k // 512, 4)
    idx = np.arange(k)
    return np.exp2(a[idx // 512, idx % 128 // 32])


BF16 = ml_dtypes.bfloat16


def bf(x):
    return np.asarray(x, np.float32).astype(BF16)


def f64(x):
    return np.asarray(x).astype(np.float64)


B, S, H, NH, HD = 1, 256, 2048, 16, 128
D = NH * HD
ROPE_BASE = 10000.0


def rope_tables():
    inv_freq = 1.0 / ROPE_BASE ** (np.arange(0, HD, 2) / HD)
    freqs = np.arange(S)[:, None] * inv_freq[None, :]
    emb = np.concatenate([freqs, freqs], axis=-1)
    return np.cos(emb), np.sin(emb)


def rotate_half(u):
    half = HD // 2
    return np.concatenate([-u[..., half:], u[..., :half]], axis=-1)


def setup_inputs():
    s = mx_kscale(H)
    sc = 1.0 / np.sqrt(H)
    return {"hidden_states": bf(np.random.standard_normal((B, S, H)) * s),
            "Wq": bf(np.random.standard_normal((D, H)) * sc / s),
            "Wk": bf(np.random.standard_normal((D, H)) * sc / s),
            "Wv": bf(np.random.standard_normal((D, H)) * sc / s)}


def reference(hidden_states, Wq, Wk, Wv):
    xq = mxq(f64(hidden_states), 2, "e4m3")

    def proj(W):
        y = xq @ mxq(f64(W), 1, "e4m3").T
        return y.reshape(B, S, NH, HD).transpose(0, 2, 1, 3)

    q, k, v = proj(Wq), proj(Wk), proj(Wv)
    cos, sin = rope_tables()
    q = q * cos + rotate_half(q) * sin
    k = k * cos + rotate_half(k) * sin
    return q, k, v

@@ -1,0 +1,194 @@
+import math
+from contextlib import ExitStack
+
+import concourse.mybir as mybir
+from concourse.masks import make_identity
+
+F32 = mybir.dt.float32
+BF16 = mybir.dt.bfloat16
+I32 = mybir.dt.int32
+U32 = mybir.dt.uint32
+U8 = mybir.dt.uint8
+FP8X4 = mybir.dt.float8_e4m3fn_x4
+ALU = mybir.AluOpType
+ACT = mybir.ActivationFunctionType
+
+P = 128
+S = 256
+H = 2048
+HEADS = 16
+HD = 128
+HALF = HD // 2
+ROPE_BASE = 10000.0
+DOUBLINGS = 6
+assert 2**DOUBLINGS == HALF
+
+K_PASS = 512
+PASSES = H // K_PASS
+WORDS_PASS = K_PASS // 2
+ROWS = 256
+BLOCKS = ROWS // P
+UNIT_HEADS = ROWS // HD
+UNITS_PER_W = HEADS // UNIT_HEADS
+
+ROUND_MAGIC = 1.5 * 2.0**23
+
+RAW_BUFS = 8
+TRANSPOSE_BANKS = 6
+SUM_BANKS = 2
+
+FLOPS = 2 * S * H * 3 * HEADS * HD
+
+
+def tile_llamaattention_pa_kernel(tc, hidden_states, Wq, Wk, Wv, out_0, out_1, out_2):
+    nc = tc.nc
+    weights = [Wq, Wk, Wv]
+    outputs = [out_0, out_1, out_2]
+    units = [(m, pair) for pair in range(UNITS_PER_W) for m in range(len(weights))]
+
+    with ExitStack() as ctx:
+        ctx.enter_context(tc.manual_schedule())
+        consts = ctx.enter_context(tc.tile_pool(name="consts", bufs=1))
+        raw_pool = ctx.enter_context(tc.tile_pool(name="raw", bufs=RAW_BUFS))
+        grouped_pool = ctx.enter_context(tc.tile_pool(name="grouped", bufs=3))
+        mx_pool = ctx.enter_context(tc.tile_pool(name="mx", bufs=3))
+        work = ctx.enter_context(tc.tile_pool(name="work", bufs=2))
+        out_pool = ctx.enter_context(tc.tile_pool(name="out", bufs=6))
+        bank_pool = ctx.enter_context(tc.psum_pool(name="banks", bufs=TRANSPOSE_BANKS))
+        sum_pool = ctx.enter_context(tc.psum_pool(name="sums", bufs=SUM_BANKS))
+
+        def load_rows(rows_view):
+            raw = raw_pool.tile([P, BLOCKS, H], BF16, name="raw")
+            nc.sync.dma_start(out=raw[:], in_=rows_view)
+            return raw
+
+        def transpose_rows(raw):
+            raw_words = raw[:].bitcast(F32)
+            grouped = grouped_pool.tile([P, PASSES, ROWS * 4], BF16, name="grouped", align_bytes=64)
+            grouped_words = grouped[:].bitcast(F32).rearrange("p g (r u) -> p g r u", u=2)
+            for g in range(PASSES):
+                bank = bank_pool.tile([P, 2, BLOCKS, P], F32, name="bank")
+                for u in range(2):
+                    first = g * WORDS_PASS + u * P
+                    for b in range(BLOCKS):
+                        nc.tensor.transpose(
+                            out=bank[:, u, b, :], in_=raw_words[:, b, first : first + P], identity=ident[:]
+                        )
+                nc.scalar.copy(out=grouped_words[:, g], in_=bank[:].rearrange("p u b r -> p (b r) u"))
+            return grouped
+
+        def quantise_rows(grouped, codes, scales):
+            nc.vector.quantize_mx(
+                out=codes[:].bitcast(FP8X4), scales=scales[:], in_=grouped[:].rearrange("p g c -> p (g c)")
+            )
+
+        def multiply(codes, scales):
+            sums = sum_pool.tile([P, 2, ROWS], F32, name="sums")
+            for e in range(2):
+                for g in range(PASSES):
+                    x_cols = slice(g * ROWS + e * P, g * ROWS + (e + 1) * P)
+                    w_cols = slice(g * ROWS, (g + 1) * ROWS)
+                    nc.tensor.matmul_mx(
+                        out=sums[:, e, :],
+                        lhsT=x_codes[:, x_cols].bitcast(FP8X4),
+                        lhsT_scale=x_scales[:, x_cols],
+                        rhs=codes[:, w_cols].bitcast(FP8X4),
+                        rhs_scale=scales[:, w_cols],
+                        start=(g == 0),
+                        stop=(g == PASSES - 1),
+                    )
+            return sums
+
+        def finish(m, pair, sums):
+            result = out_pool.tile([P, UNIT_HEADS, 2, HD], F32, name="result")
+            if m == 2:
+                nc.scalar.copy(
+                    out=result[:].rearrange("p h e f -> p e h f"),
+                    in_=sums[:].rearrange("p e (h f) -> p e h f", f=HD),
+                )
+            else:
+                halves = [P, 2, UNIT_HEADS * 2, HALF]
+                sums_halves = sums[:].rearrange("p e (c j) -> p e c j", j=HALF)
+                by_cos = work.tile(halves, F32, name="by_cos")
+                by_sin = work.tile(halves, F32, name="by_sin")
+                nc.vector.tensor_tensor(
+                    out=by_cos[:], in0=sums_halves, in1=cos_sin[:, :, 0, :].unsqueeze(2).to_broadcast(halves), op=ALU.mult
+                )
+                nc.vector.tensor_tensor(
+                    out=by_sin[:], in0=sums_halves, in1=cos_sin[:, :, 1, :].unsqueeze(2).to_broadcast(halves), op=ALU.mult
+                )
+                c = by_cos[:].rearrange("p e (h t) j -> p e h t j", t=2)
+                s = by_sin[:].rearrange("p e (h t) j -> p e h t j", t=2)
+                r = result[:].rearrange("p h e (t j) -> p e h t j", t=2)
+                nc.vector.tensor_tensor(out=r[:, :, :, 0, :], in0=c[:, :, :, 0, :], in1=s[:, :, :, 1, :], op=ALU.subtract)
+                nc.vector.tensor_tensor(out=r[:, :, :, 1, :], in0=c[:, :, :, 1, :], in1=s[:, :, :, 0, :], op=ALU.add)
+            first_head = pair * UNIT_HEADS
+            nc.sync.dma_start(
+                out=outputs[m][0, first_head : first_head + UNIT_HEADS].rearrange("h (p e) f -> p h (e f)", e=2),
+                in_=result[:].rearrange("p h e f -> p h (e f)"),
+            )
+
+        def weight_rows(u):
+            m, pair = units[u]
+            return weights[m][pair * ROWS : (pair + 1) * ROWS, :].rearrange("(b p) k -> p b k", p=P)
+
+        x_raw = load_rows(hidden_states[0].rearrange("(p e) k -> p e k", e=2))
+        raws = {}
+        for u in range(RAW_BUFS - 1):
+            raws[u] = load_rows(weight_rows(u))
+
+        ident = consts.tile([P, P], F32, name="ident")
+        make_identity(nc, ident[:])
+        position_int = consts.tile([P, 2], I32, name="position_int")
+        nc.gpsimd.iota(position_int[:], pattern=[[1, 2]], base=0, channel_multiplier=2)
+        position_turns = consts.tile([P, 2], F32, name="position_turns")
+        nc.vector.tensor_scalar_mul(out=position_turns[:], in0=position_int[:], scalar1=1.0 / (2.0 * math.pi))
+
+        inv_freq = consts.tile([P, HALF], F32, name="inv_freq")
+        nc.vector.memset(inv_freq[:, 0:1], 1.0)
+        for doubling in range(DOUBLINGS):
+            width = 2**doubling
+            nc.vector.tensor_scalar_mul(
+                out=inv_freq[:, width : 2 * width],
+                in0=inv_freq[:, 0:width],
+                scalar1=ROPE_BASE ** (-width / HALF),
+            )
+
+        turns = consts.tile([P, 2, 2, HALF], F32, name="turns")
+        for e in range(2):
+            nc.vector.tensor_scalar(
+                out=turns[:, e, 0, :], in0=inv_freq[:], scalar1=position_turns[:, e : e + 1], scalar2=0.25,
+                op0=ALU.mult, op1=ALU.add,
+            )
+            nc.vector.tensor_scalar_mul(out=turns[:, e, 1, :], in0=inv_freq[:], scalar1=position_turns[:, e : e + 1])
+        whole_turns = consts.tile([P, 2, 2, HALF], F32, name="whole_turns")
+        nc.vector.tensor_scalar(
+            out=whole_turns[:], in0=turns[:], scalar1=ROUND_MAGIC, scalar2=ROUND_MAGIC, op0=ALU.add, op1=ALU.subtract
+        )
+        part_turns = consts.tile([P, 2, 2, HALF], F32, name="part_turns")
+        nc.vector.tensor_tensor(out=part_turns[:], in0=turns[:], in1=whole_turns[:], op=ALU.subtract)
+        cos_sin = consts.tile([P, 2, 2, HALF], F32, name="cos_sin")
+        nc.scalar.activation(out=cos_sin[:], in_=part_turns[:], func=ACT.Sin, scale=2.0 * math.pi)
+
+        x_codes = consts.tile([P, PASSES * ROWS], U32, name="x_codes", align_bytes=64)
+        x_scales = consts.tile([P, PASSES * ROWS], U8, name="x_scales", align_bytes=64)
+        quantise_rows(transpose_rows(x_raw), x_codes, x_scales)
+
+        groupeds, mx_tiles, sums_of = {}, {}, {}
+        for step in range(len(units) + 3):
+            if 0 <= step - 3:
+                m, pair = units[step - 3]
+                finish(m, pair, sums_of[step - 3])
+            if step < len(units):
+                groupeds[step] = transpose_rows(raws[step])
+            ahead = step + RAW_BUFS - 1
+            if ahead < len(units):
+                raws[ahead] = load_rows(weight_rows(ahead))
+            if 0 <= step - 2 < len(units):
+                codes, scales = mx_tiles[step - 2]
+                sums_of[step - 2] = multiply(codes, scales)
+            if 0 <= step - 1 < len(units):
+                codes = mx_pool.tile([P, PASSES * ROWS], U32, name="codes", align_bytes=64)
+                scales = mx_pool.tile([P, PASSES * ROWS], U8, name="scales", align_bytes=64)
+                quantise_rows(groupeds[step - 1], codes, scales)
+                mx_tiles[step - 1] = (codes, scales)

@@ -62,10 +62,10 @@ def tile_llamaattention_pa_kernel(tc, hidden_states, Wq, Wk, Wv, out_0, out_1, o
             nc.sync.dma_start(out=raw[:], in_=rows_view)
             return raw
 
-        def transpose_rows(raw):
+        def transpose_rows(raw, column_order):
             raw_words = raw[:].bitcast(F32)
             grouped = grouped_pool.tile([P, PASSES, ROWS * 4], BF16, name="grouped", align_bytes=64)
-            grouped_words = grouped[:].bitcast(F32).rearrange("p g (r u) -> p g r u", u=2)
+            grouped_words = grouped[:].bitcast(F32)
             for g in range(PASSES):
                 bank = bank_pool.tile([P, 2, BLOCKS, P], F32, name="bank")
                 for u in range(2):
@@ -74,7 +74,10 @@ def tile_llamaattention_pa_kernel(tc, hidden_states, Wq, Wk, Wv, out_0, out_1, o
                         nc.tensor.transpose(
                             out=bank[:, u, b, :], in_=raw_words[:, b, first : first + P], identity=ident[:]
                         )
-                nc.scalar.copy(out=grouped_words[:, g], in_=bank[:].rearrange("p u b r -> p (b r) u"))
+                nc.scalar.copy(
+                    out=grouped_words[:, g].rearrange("p (%s u) -> p %s u" % (column_order, column_order), b=BLOCKS, u=2),
+                    in_=bank[:].rearrange("p u b r -> p %s u" % column_order),
+                )
             return grouped
 
         def quantise_rows(grouped, codes, scales):
@@ -130,7 +133,7 @@ def tile_llamaattention_pa_kernel(tc, hidden_states, Wq, Wk, Wv, out_0, out_1, o
 
         def weight_rows(u):
             m, pair = units[u]
-            return weights[m][pair * ROWS : (pair + 1) * ROWS, :].rearrange("(b p) k -> p b k", p=P)
+            return weights[m][pair * ROWS : (pair + 1) * ROWS, :].rearrange("(p b) k -> p b k", b=BLOCKS)
 
         x_raw = load_rows(hidden_states[0].rearrange("(p e) k -> p e k", e=2))
         raws = {}
@@ -172,7 +175,7 @@ def tile_llamaattention_pa_kernel(tc, hidden_states, Wq, Wk, Wv, out_0, out_1, o
 
         x_codes = consts.tile([P, PASSES * ROWS], U32, name="x_codes", align_bytes=64)
         x_scales = consts.tile([P, PASSES * ROWS], U8, name="x_scales", align_bytes=64)
-        quantise_rows(transpose_rows(x_raw), x_codes, x_scales)
+        quantise_rows(transpose_rows(x_raw, "b r"), x_codes, x_scales)
 
         groupeds, mx_tiles, sums_of = {}, {}, {}
         for step in range(len(units) + 3):
@@ -180,7 +183,7 @@ def tile_llamaattention_pa_kernel(tc, hidden_states, Wq, Wk, Wv, out_0, out_1, o
                 m, pair = units[step - 3]
                 finish(m, pair, sums_of[step - 3])
             if step < len(units):
-                groupeds[step] = transpose_rows(raws[step])
+                groupeds[step] = transpose_rows(raws[step], "r b")
             ahead = step + RAW_BUFS - 1
             if ahead < len(units):
                 raws[ahead] = load_rows(weight_rows(ahead))

@@ -53,7 +53,7 @@ def tile_llamaattention_pa_kernel(tc, hidden_states, Wq, Wk, Wv, out_0, out_1, o
         grouped_pool = ctx.enter_context(tc.tile_pool(name="grouped", bufs=3))
         mx_pool = ctx.enter_context(tc.tile_pool(name="mx", bufs=3))
         work = ctx.enter_context(tc.tile_pool(name="work", bufs=2))
-        out_pool = ctx.enter_context(tc.tile_pool(name="out", bufs=6))
+        out_pool = ctx.enter_context(tc.tile_pool(name="out", bufs=len(units)))
         bank_pool = ctx.enter_context(tc.psum_pool(name="banks", bufs=TRANSPOSE_BANKS))
         sum_pool = ctx.enter_context(tc.psum_pool(name="sums", bufs=SUM_BANKS))
 
@@ -125,6 +125,9 @@ def tile_llamaattention_pa_kernel(tc, hidden_states, Wq, Wk, Wv, out_0, out_1, o
                 r = result[:].rearrange("p h e (t j) -> p e h t j", t=2)
                 nc.vector.tensor_tensor(out=r[:, :, :, 0, :], in0=c[:, :, :, 0, :], in1=s[:, :, :, 1, :], op=ALU.subtract)
                 nc.vector.tensor_tensor(out=r[:, :, :, 1, :], in0=c[:, :, :, 1, :], in1=s[:, :, :, 0, :], op=ALU.add)
+            return result
+
+        def store(m, pair, result):
             first_head = pair * UNIT_HEADS
             nc.sync.dma_start(
                 out=outputs[m][0, first_head : first_head + UNIT_HEADS].rearrange("h (p e) f -> p h (e f)", e=2),
@@ -178,15 +181,20 @@ def tile_llamaattention_pa_kernel(tc, hidden_states, Wq, Wk, Wv, out_0, out_1, o
         quantise_rows(transpose_rows(x_raw, "b r"), x_codes, x_scales)
 
         groupeds, mx_tiles, sums_of = {}, {}, {}
+        finished = []
         for step in range(len(units) + 3):
             if 0 <= step - 3:
                 m, pair = units[step - 3]
-                finish(m, pair, sums_of[step - 3])
+                finished.append((m, pair, finish(m, pair, sums_of[step - 3])))
             if step < len(units):
                 groupeds[step] = transpose_rows(raws[step], "r b")
             ahead = step + RAW_BUFS - 1
             if ahead < len(units):
                 raws[ahead] = load_rows(weight_rows(ahead))
+            if ahead >= len(units) - 1:
+                for m, pair, result in finished:
+                    store(m, pair, result)
+                finished.clear()
             if 0 <= step - 2 < len(units):
                 codes, scales = mx_tiles[step - 2]
                 sums_of[step - 2] = multiply(codes, scales)

@@ -52,7 +52,7 @@ def tile_llamaattention_pa_kernel(tc, hidden_states, Wq, Wk, Wv, out_0, out_1, o
         raw_pool = ctx.enter_context(tc.tile_pool(name="raw", bufs=RAW_BUFS))
         grouped_pool = ctx.enter_context(tc.tile_pool(name="grouped", bufs=3))
         mx_pool = ctx.enter_context(tc.tile_pool(name="mx", bufs=3))
-        work = ctx.enter_context(tc.tile_pool(name="work", bufs=2))
+        work = ctx.enter_context(tc.tile_pool(name="work", bufs=3))
         out_pool = ctx.enter_context(tc.tile_pool(name="out", bufs=len(units)))
         bank_pool = ctx.enter_context(tc.psum_pool(name="banks", bufs=TRANSPOSE_BANKS))
         sum_pool = ctx.enter_context(tc.psum_pool(name="sums", bufs=SUM_BANKS))
@@ -123,8 +123,8 @@ def tile_llamaattention_pa_kernel(tc, hidden_states, Wq, Wk, Wv, out_0, out_1, o
                 c = by_cos[:].rearrange("p e (h t) j -> p e h t j", t=2)
                 s = by_sin[:].rearrange("p e (h t) j -> p e h t j", t=2)
                 r = result[:].rearrange("p h e (t j) -> p e h t j", t=2)
-                nc.vector.tensor_tensor(out=r[:, :, :, 0, :], in0=c[:, :, :, 0, :], in1=s[:, :, :, 1, :], op=ALU.subtract)
-                nc.vector.tensor_tensor(out=r[:, :, :, 1, :], in0=c[:, :, :, 1, :], in1=s[:, :, :, 0, :], op=ALU.add)
+                nc.gpsimd.tensor_tensor(out=r[:, :, :, 0, :], in0=c[:, :, :, 0, :], in1=s[:, :, :, 1, :], op=ALU.subtract)
+                nc.gpsimd.tensor_tensor(out=r[:, :, :, 1, :], in0=c[:, :, :, 1, :], in1=s[:, :, :, 0, :], op=ALU.add)
             return result
 
         def store(m, pair, result):

@@ -105,7 +105,7 @@ def tile_llamaattention_pa_kernel(tc, hidden_states, Wq, Wk, Wv, out_0, out_1, o
         def finish(m, pair, sums):
             result = out_pool.tile([P, UNIT_HEADS, 2, HD], F32, name="result")
             if m == 2:
-                nc.scalar.copy(
+                nc.vector.tensor_copy(
                     out=result[:].rearrange("p h e f -> p e h f"),
                     in_=sums[:].rearrange("p e (h f) -> p e h f", f=HD),
                 )

@@ -44,7 +44,7 @@ def tile_llamaattention_pa_kernel(tc, hidden_states, Wq, Wk, Wv, out_0, out_1, o
     nc = tc.nc
     weights = [Wq, Wk, Wv]
     outputs = [out_0, out_1, out_2]
-    units = [(m, pair) for pair in range(UNITS_PER_W) for m in range(len(weights))]
+    units = [(m, pair) for pair in range(UNITS_PER_W) for m in (0, 1)] + [(2, pair) for pair in range(UNITS_PER_W)]
 
     with ExitStack() as ctx:
         ctx.enter_context(tc.manual_schedule())
@@ -80,10 +80,14 @@ def tile_llamaattention_pa_kernel(tc, hidden_states, Wq, Wk, Wv, out_0, out_1, o
                 )
             return grouped
 
-        def quantise_rows(grouped, codes, scales):
-            nc.vector.quantize_mx(
-                out=codes[:].bitcast(FP8X4), scales=scales[:], in_=grouped[:].rearrange("p g c -> p (g c)")
-            )
+        def quantise_rows(grouped, codes, scales, calls=1):
+            flat = grouped[:].rearrange("p g c -> p (g c)")
+            width = PASSES * ROWS // calls
+            for call in range(calls):
+                cols = slice(call * width, (call + 1) * width)
+                nc.vector.quantize_mx(
+                    out=codes[:, cols].bitcast(FP8X4), scales=scales[:, cols], in_=flat[:, 4 * cols.start : 4 * cols.stop]
+                )
 
         def multiply(codes, scales):
             sums = sum_pool.tile([P, 2, ROWS], F32, name="sums")
@@ -182,7 +186,17 @@ def tile_llamaattention_pa_kernel(tc, hidden_states, Wq, Wk, Wv, out_0, out_1, o
 
         groupeds, mx_tiles, sums_of = {}, {}, {}
         finished = []
+        last = len(units) - 1
+
+        def quantise_unit(u, calls):
+            codes = mx_pool.tile([P, PASSES * ROWS], U32, name="codes", align_bytes=64)
+            scales = mx_pool.tile([P, PASSES * ROWS], U8, name="scales", align_bytes=64)
+            quantise_rows(groupeds[u], codes, scales, calls)
+            mx_tiles[u] = (codes, scales)
+
         for step in range(len(units) + 3):
+            if step - 1 == last:
+                quantise_unit(last, PASSES)
             if 0 <= step - 3:
                 m, pair = units[step - 3]
                 finished.append((m, pair, finish(m, pair, sums_of[step - 3])))
@@ -198,8 +212,5 @@ def tile_llamaattention_pa_kernel(tc, hidden_states, Wq, Wk, Wv, out_0, out_1, o
             if 0 <= step - 2 < len(units):
                 codes, scales = mx_tiles[step - 2]
                 sums_of[step - 2] = multiply(codes, scales)
-            if 0 <= step - 1 < len(units):
-                codes = mx_pool.tile([P, PASSES * ROWS], U32, name="codes", align_bytes=64)
-                scales = mx_pool.tile([P, PASSES * ROWS], U8, name="scales", align_bytes=64)
-                quantise_rows(groupeds[step - 1], codes, scales)
-                mx_tiles[step - 1] = (codes, scales)
+            if 0 <= step - 1 < last:
+                quantise_unit(step - 1, 1)

@@ -140,7 +140,7 @@ def tile_llamaattention_pa_kernel(tc, hidden_states, Wq, Wk, Wv, out_0, out_1, o
 
         def weight_rows(u):
             m, pair = units[u]
-            return weights[m][pair * ROWS : (pair + 1) * ROWS, :].rearrange("(p b) k -> p b k", b=BLOCKS)
+            return weights[m][pair * ROWS : (pair + 1) * ROWS, :].rearrange("(b p) k -> p b k", p=P)
 
         x_raw = load_rows(hidden_states[0].rearrange("(p e) k -> p e k", e=2))
         raws = {}
@@ -201,7 +201,7 @@ def tile_llamaattention_pa_kernel(tc, hidden_states, Wq, Wk, Wv, out_0, out_1, o
                 m, pair = units[step - 3]
                 finished.append((m, pair, finish(m, pair, sums_of[step - 3])))
             if step < len(units):
-                groupeds[step] = transpose_rows(raws[step], "r b")
+                groupeds[step] = transpose_rows(raws[step], "b r")
             ahead = step + RAW_BUFS - 1
             if ahead < len(units):
                 raws[ahead] = load_rows(weight_rows(ahead))

@@ -36,6 +36,7 @@ ROUND_MAGIC = 1.5 * 2.0**23
 RAW_BUFS = 8
 TRANSPOSE_BANKS = 6
 SUM_BANKS = 2
+SINGLE_RUNS = 4
 
 FLOPS = 2 * S * H * 3 * HEADS * HD
 
@@ -50,8 +51,8 @@ def tile_llamaattention_pa_kernel(tc, hidden_states, Wq, Wk, Wv, out_0, out_1, o
         ctx.enter_context(tc.manual_schedule())
         consts = ctx.enter_context(tc.tile_pool(name="consts", bufs=1))
         raw_pool = ctx.enter_context(tc.tile_pool(name="raw", bufs=RAW_BUFS))
-        grouped_pool = ctx.enter_context(tc.tile_pool(name="grouped", bufs=3))
-        mx_pool = ctx.enter_context(tc.tile_pool(name="mx", bufs=3))
+        grouped_pool = ctx.enter_context(tc.tile_pool(name="grouped", bufs=5))
+        mx_pool = ctx.enter_context(tc.tile_pool(name="mx", bufs=5))
         work = ctx.enter_context(tc.tile_pool(name="work", bufs=3))
         out_pool = ctx.enter_context(tc.tile_pool(name="out", bufs=len(units)))
         bank_pool = ctx.enter_context(tc.psum_pool(name="banks", bufs=TRANSPOSE_BANKS))
@@ -184,33 +185,40 @@ def tile_llamaattention_pa_kernel(tc, hidden_states, Wq, Wk, Wv, out_0, out_1, o
         x_scales = consts.tile([P, PASSES * ROWS], U8, name="x_scales", align_bytes=64)
         quantise_rows(transpose_rows(x_raw, "b r"), x_codes, x_scales)
 
-        groupeds, mx_tiles, sums_of = {}, {}, {}
-        finished = []
-        last = len(units) - 1
-
-        def quantise_unit(u, calls):
-            codes = mx_pool.tile([P, PASSES * ROWS], U32, name="codes", align_bytes=64)
-            scales = mx_pool.tile([P, PASSES * ROWS], U8, name="scales", align_bytes=64)
-            quantise_rows(groupeds[u], codes, scales, calls)
-            mx_tiles[u] = (codes, scales)
-
-        for step in range(len(units) + 3):
-            if step - 1 == last:
-                quantise_unit(last, PASSES)
-            if 0 <= step - 3:
-                m, pair = units[step - 3]
-                finished.append((m, pair, finish(m, pair, sums_of[step - 3])))
-            if step < len(units):
-                groupeds[step] = transpose_rows(raws[step], "b r")
-            ahead = step + RAW_BUFS - 1
-            if ahead < len(units):
-                raws[ahead] = load_rows(weight_rows(ahead))
-            if ahead >= len(units) - 1:
-                for m, pair, result in finished:
-                    store(m, pair, result)
-                finished.clear()
-            if 0 <= step - 2 < len(units):
-                codes, scales = mx_tiles[step - 2]
-                sums_of[step - 2] = multiply(codes, scales)
-            if 0 <= step - 1 < last:
-                quantise_unit(step - 1, 1)
+        n_units = len(units)
+        last = n_units - 1
+        runs = [[u] for u in range(SINGLE_RUNS)] + [[u, u + 1] for u in range(SINGLE_RUNS, n_units, 2)] + [[]]
+        groupeds, sums_of = {}, {}
+        results = []
+        loaded = RAW_BUFS - 1
+        multiplied = 0
+        stored = 0
+        for run in runs:
+            for u in run:
+                groupeds[u] = transpose_rows(raws[u], "b r")
+                if loaded < n_units:
+                    raws[loaded] = load_rows(weight_rows(loaded))
+                    loaded += 1
+            if len(run) == 2:
+                ready = run[0]
+            elif len(run) == 1:
+                ready = max(run[0] - 1, 0)
+            else:
+                ready = n_units
+            for u in range(multiplied, ready):
+                codes = mx_pool.tile([P, PASSES * ROWS], U32, name="codes", align_bytes=64)
+                scales = mx_pool.tile([P, PASSES * ROWS], U8, name="scales", align_bytes=64)
+                quantise_rows(groupeds[u], codes, scales, PASSES if u == last else 1)
+                if u >= 2:
+                    m, pair = units[u - 2]
+                    results.append(finish(m, pair, sums_of[u - 2]))
+                sums_of[u] = multiply(codes, scales)
+            multiplied = ready
+            if loaded == n_units:
+                while stored < len(results):
+                    m, pair = units[stored]
+                    store(m, pair, results[stored])
+                    stored += 1
+        for u in range(n_units - 2, n_units):
+            m, pair = units[u]
+            store(m, pair, finish(m, pair, sums_of[u]))

@@ -116,20 +116,29 @@ def tile_llamaattention_pa_kernel(tc, hidden_states, Wq, Wk, Wv, out_0, out_1, o
                 )
             else:
                 halves = [P, 2, UNIT_HEADS * 2, HALF]
-                sums_halves = sums[:].rearrange("p e (c j) -> p e c j", j=HALF)
+                half = [P, 2, UNIT_HEADS, HALF]
                 by_cos = work.tile(halves, F32, name="by_cos")
-                by_sin = work.tile(halves, F32, name="by_sin")
+                turned = work.tile(halves, F32, name="turned")
                 nc.vector.tensor_tensor(
-                    out=by_cos[:], in0=sums_halves, in1=cos_sin[:, :, 0, :].unsqueeze(2).to_broadcast(halves), op=ALU.mult
+                    out=by_cos[:],
+                    in0=sums[:].rearrange("p e (c j) -> p e c j", j=HALF),
+                    in1=cos_sin[:, :, 0, :].unsqueeze(2).to_broadcast(halves),
+                    op=ALU.mult,
+                )
+                y = sums[:].rearrange("p e (h t j) -> p e h t j", t=2, j=HALF)
+                w = turned[:].rearrange("p e (h t) j -> p e h t j", t=2)
+                nc.vector.tensor_tensor(
+                    out=w[:, :, :, 0, :], in0=y[:, :, :, 1, :], in1=minus_sin[:].unsqueeze(2).to_broadcast(half), op=ALU.mult
                 )
                 nc.vector.tensor_tensor(
-                    out=by_sin[:], in0=sums_halves, in1=cos_sin[:, :, 1, :].unsqueeze(2).to_broadcast(halves), op=ALU.mult
+                    out=w[:, :, :, 1, :], in0=y[:, :, :, 0, :], in1=cos_sin[:, :, 1, :].unsqueeze(2).to_broadcast(half), op=ALU.mult
                 )
-                c = by_cos[:].rearrange("p e (h t) j -> p e h t j", t=2)
-                s = by_sin[:].rearrange("p e (h t) j -> p e h t j", t=2)
-                r = result[:].rearrange("p h e (t j) -> p e h t j", t=2)
-                nc.gpsimd.tensor_tensor(out=r[:, :, :, 0, :], in0=c[:, :, :, 0, :], in1=s[:, :, :, 1, :], op=ALU.subtract)
-                nc.gpsimd.tensor_tensor(out=r[:, :, :, 1, :], in0=c[:, :, :, 1, :], in1=s[:, :, :, 0, :], op=ALU.add)
+                nc.gpsimd.tensor_tensor(
+                    out=result[:].rearrange("p h e f -> p e h f"),
+                    in0=by_cos[:].rearrange("p e (h t) j -> p e h (t j)", t=2),
+                    in1=turned[:].rearrange("p e (h t) j -> p e h (t j)", t=2),
+                    op=ALU.add,
+                )
             return result
 
         def store(m, pair, result):
@@ -180,6 +189,8 @@ def tile_llamaattention_pa_kernel(tc, hidden_states, Wq, Wk, Wv, out_0, out_1, o
         nc.vector.tensor_tensor(out=part_turns[:], in0=turns[:], in1=whole_turns[:], op=ALU.subtract)
         cos_sin = consts.tile([P, 2, 2, HALF], F32, name="cos_sin")
         nc.scalar.activation(out=cos_sin[:], in_=part_turns[:], func=ACT.Sin, scale=2.0 * math.pi)
+        minus_sin = consts.tile([P, 2, HALF], F32, name="minus_sin")
+        nc.vector.tensor_scalar_mul(out=minus_sin[:], in0=cos_sin[:, :, 1, :], scalar1=-1.0)
 
         x_codes = consts.tile([P, PASSES * ROWS], U32, name="x_codes", align_bytes=64)
         x_scales = consts.tile([P, PASSES * ROWS], U8, name="x_scales", align_bytes=64)

@@ -33,9 +33,11 @@ UNITS_PER_W = HEADS // UNIT_HEADS
 
 ROUND_MAGIC = 1.5 * 2.0**23
 
-RAW_BUFS = 8
+RAW_BUFS = 5
+JOINED_FROM = 5
 TRANSPOSE_BANKS = 6
 SUM_BANKS = 2
+STORE_UNITS = 4
 SINGLE_RUNS = 4
 
 FLOPS = 2 * S * H * 3 * HEADS * HD
@@ -45,7 +47,8 @@ def tile_llamaattention_pa_kernel(tc, hidden_states, Wq, Wk, Wv, out_0, out_1, o
     nc = tc.nc
     weights = [Wq, Wk, Wv]
     outputs = [out_0, out_1, out_2]
-    units = [(m, pair) for pair in range(UNITS_PER_W) for m in (0, 1)] + [(2, pair) for pair in range(UNITS_PER_W)]
+    units = [(m, first + d) for first in range(0, UNITS_PER_W, 2) for m in (0, 1) for d in (0, 1)]
+    units += [(2, pair) for pair in range(UNITS_PER_W)]
 
     with ExitStack() as ctx:
         ctx.enter_context(tc.manual_schedule())
@@ -54,17 +57,25 @@ def tile_llamaattention_pa_kernel(tc, hidden_states, Wq, Wk, Wv, out_0, out_1, o
         grouped_pool = ctx.enter_context(tc.tile_pool(name="grouped", bufs=5))
         mx_pool = ctx.enter_context(tc.tile_pool(name="mx", bufs=5))
         work = ctx.enter_context(tc.tile_pool(name="work", bufs=3))
-        out_pool = ctx.enter_context(tc.tile_pool(name="out", bufs=len(units)))
+        out_pool = ctx.enter_context(tc.tile_pool(name="out", bufs=len(units) // STORE_UNITS))
         bank_pool = ctx.enter_context(tc.psum_pool(name="banks", bufs=TRANSPOSE_BANKS))
         sum_pool = ctx.enter_context(tc.psum_pool(name="sums", bufs=SUM_BANKS))
 
-        def load_rows(rows_view):
-            raw = raw_pool.tile([P, BLOCKS, H], BF16, name="raw")
-            nc.sync.dma_start(out=raw[:], in_=rows_view)
-            return raw
+        def load_tile(t):
+            m, pair = units[2 * t]
+            rows = weights[m][pair * ROWS : (pair + 2) * ROWS, :].rearrange("(c p) k -> p c k", p=P)
+            raw = raw_pool.tile([P, 2 * BLOCKS, H], BF16, name="raw")
+            if t >= JOINED_FROM:
+                nc.sync.dma_start(out=raw[:], in_=rows)
+            else:
+                for d in range(2):
+                    blocks = slice(d * BLOCKS, (d + 1) * BLOCKS)
+                    nc.sync.dma_start(out=raw[:, blocks, :], in_=rows[:, blocks, :])
+            for d in range(2):
+                raws[2 * t + d] = raw[:, d * BLOCKS : (d + 1) * BLOCKS, :]
 
         def transpose_rows(raw, column_order):
-            raw_words = raw[:].bitcast(F32)
+            raw_words = raw.bitcast(F32)
             grouped = grouped_pool.tile([P, PASSES, ROWS * 4], BF16, name="grouped", align_bytes=64)
             grouped_words = grouped[:].bitcast(F32)
             for g in range(PASSES):
@@ -107,11 +118,18 @@ def tile_llamaattention_pa_kernel(tc, hidden_states, Wq, Wk, Wv, out_0, out_1, o
                     )
             return sums
 
+        shared = {}
+        to_store = []
+
         def finish(m, pair, sums):
-            result = out_pool.tile([P, UNIT_HEADS, 2, HD], F32, name="result")
+            group = (m, pair // STORE_UNITS)
+            if group not in shared:
+                shared[group] = out_pool.tile([P, STORE_UNITS * UNIT_HEADS, 2, HD], F32, name="result")
+            first_head = (pair % STORE_UNITS) * UNIT_HEADS
+            result = shared[group][:, first_head : first_head + UNIT_HEADS]
             if m == 2:
                 nc.vector.tensor_copy(
-                    out=result[:].rearrange("p h e f -> p e h f"),
+                    out=result.rearrange("p h e f -> p e h f"),
                     in_=sums[:].rearrange("p e (h f) -> p e h f", f=HD),
                 )
             else:
@@ -134,28 +152,30 @@ def tile_llamaattention_pa_kernel(tc, hidden_states, Wq, Wk, Wv, out_0, out_1, o
                     out=w[:, :, :, 1, :], in0=y[:, :, :, 0, :], in1=cos_sin[:, :, 1, :].unsqueeze(2).to_broadcast(half), op=ALU.mult
                 )
                 nc.gpsimd.tensor_tensor(
-                    out=result[:].rearrange("p h e f -> p e h f"),
+                    out=result.rearrange("p h e f -> p e h f"),
                     in0=by_cos[:].rearrange("p e (h t) j -> p e h (t j)", t=2),
                     in1=turned[:].rearrange("p e (h t) j -> p e h (t j)", t=2),
                     op=ALU.add,
                 )
-            return result
+            if group == (2, UNITS_PER_W // STORE_UNITS - 1):
+                to_store.append((m, pair, 1))
+            elif pair % STORE_UNITS == STORE_UNITS - 1:
+                to_store.append((m, pair - (STORE_UNITS - 1), STORE_UNITS))
 
-        def store(m, pair, result):
-            first_head = pair * UNIT_HEADS
+        def store(m, first_pair, count):
+            heads = count * UNIT_HEADS
+            first_head = first_pair * UNIT_HEADS
+            in_tile = (first_pair % STORE_UNITS) * UNIT_HEADS
             nc.sync.dma_start(
-                out=outputs[m][0, first_head : first_head + UNIT_HEADS].rearrange("h (p e) f -> p h (e f)", e=2),
-                in_=result[:].rearrange("p h e f -> p h (e f)"),
+                out=outputs[m][0, first_head : first_head + heads].rearrange("h (p e) f -> p h (e f)", e=2),
+                in_=shared[(m, first_pair // STORE_UNITS)][:, in_tile : in_tile + heads].rearrange("p h e f -> p h (e f)"),
             )
 
-        def weight_rows(u):
-            m, pair = units[u]
-            return weights[m][pair * ROWS : (pair + 1) * ROWS, :].rearrange("(b p) k -> p b k", p=P)
-
-        x_raw = load_rows(hidden_states[0].rearrange("(p e) k -> p e k", e=2))
+        x_raw = consts.tile([P, BLOCKS, H], BF16, name="x_raw")
+        nc.sync.dma_start(out=x_raw[:], in_=hidden_states[0].rearrange("(p e) k -> p e k", e=2))
         raws = {}
-        for u in range(RAW_BUFS - 1):
-            raws[u] = load_rows(weight_rows(u))
+        for t in range(RAW_BUFS):
+            load_tile(t)
 
         ident = consts.tile([P, P], F32, name="ident")
         make_identity(nc, ident[:])
@@ -194,21 +214,20 @@ def tile_llamaattention_pa_kernel(tc, hidden_states, Wq, Wk, Wv, out_0, out_1, o
 
         x_codes = consts.tile([P, PASSES * ROWS], U32, name="x_codes", align_bytes=64)
         x_scales = consts.tile([P, PASSES * ROWS], U8, name="x_scales", align_bytes=64)
-        quantise_rows(transpose_rows(x_raw, "b r"), x_codes, x_scales)
+        quantise_rows(transpose_rows(x_raw[:], "b r"), x_codes, x_scales)
 
         n_units = len(units)
         last = n_units - 1
         runs = [[u] for u in range(SINGLE_RUNS)] + [[u, u + 1] for u in range(SINGLE_RUNS, n_units, 2)] + [[]]
         groupeds, sums_of = {}, {}
-        results = []
-        loaded = RAW_BUFS - 1
+        n_tiles = n_units // 2
+        loaded = RAW_BUFS
         multiplied = 0
-        stored = 0
         for run in runs:
             for u in run:
                 groupeds[u] = transpose_rows(raws[u], "b r")
-                if loaded < n_units:
-                    raws[loaded] = load_rows(weight_rows(loaded))
+                if u % 2 == 1 and loaded < n_tiles:
+                    load_tile(loaded)
                     loaded += 1
             if len(run) == 2:
                 ready = run[0]
@@ -222,14 +241,16 @@ def tile_llamaattention_pa_kernel(tc, hidden_states, Wq, Wk, Wv, out_0, out_1, o
                 quantise_rows(groupeds[u], codes, scales, PASSES if u == last else 1)
                 if u >= 2:
                     m, pair = units[u - 2]
-                    results.append(finish(m, pair, sums_of[u - 2]))
+                    finish(m, pair, sums_of[u - 2])
                 sums_of[u] = multiply(codes, scales)
             multiplied = ready
-            if loaded == n_units:
-                while stored < len(results):
-                    m, pair = units[stored]
-                    store(m, pair, results[stored])
-                    stored += 1
+            if loaded == n_tiles:
+                for m, first_pair, count in to_store:
+                    store(m, first_pair, count)
+                to_store.clear()
         for u in range(n_units - 2, n_units):
             m, pair = units[u]
-            store(m, pair, finish(m, pair, sums_of[u]))
+            finish(m, pair, sums_of[u])
+            for m, first_pair, count in to_store:
+                store(m, first_pair, count)
+            to_store.clear()

@@ -101,8 +101,13 @@ def tile_llamaattention_pa_kernel(tc, hidden_states, Wq, Wk, Wv, out_0, out_1, o
                     out=codes[:, cols].bitcast(FP8X4), scales=scales[:, cols], in_=flat[:, 4 * cols.start : 4 * cols.stop]
                 )
 
-        def multiply(codes, scales):
-            sums = sum_pool.tile([P, 2, ROWS], F32, name="sums")
+        def multiply(codes, scales, in_transpose_bank):
+            if in_transpose_bank:
+                bank = bank_pool.tile([P, 2, BLOCKS, P], F32, name="bank")
+                sums = bank[:].rearrange("p u b r -> p u (b r)")
+            else:
+                sum_bank = sum_pool.tile([P, 2, ROWS], F32, name="sum_bank")
+                sums = sum_bank[:]
             for e in range(2):
                 for g in range(PASSES):
                     x_cols = slice(g * ROWS + e * P, g * ROWS + (e + 1) * P)
@@ -130,7 +135,7 @@ def tile_llamaattention_pa_kernel(tc, hidden_states, Wq, Wk, Wv, out_0, out_1, o
             if m == 2:
                 nc.vector.tensor_copy(
                     out=result.rearrange("p h e f -> p e h f"),
-                    in_=sums[:].rearrange("p e (h f) -> p e h f", f=HD),
+                    in_=sums.rearrange("p e (h f) -> p e h f", f=HD),
                 )
             else:
                 halves = [P, 2, UNIT_HEADS * 2, HALF]
@@ -139,11 +144,11 @@ def tile_llamaattention_pa_kernel(tc, hidden_states, Wq, Wk, Wv, out_0, out_1, o
                 turned = work.tile(halves, F32, name="turned")
                 nc.vector.tensor_tensor(
                     out=by_cos[:],
-                    in0=sums[:].rearrange("p e (c j) -> p e c j", j=HALF),
+                    in0=sums.rearrange("p e (c j) -> p e c j", j=HALF),
                     in1=cos_sin[:, :, 0, :].unsqueeze(2).to_broadcast(halves),
                     op=ALU.mult,
                 )
-                y = sums[:].rearrange("p e (h t j) -> p e h t j", t=2, j=HALF)
+                y = sums.rearrange("p e (h t j) -> p e h t j", t=2, j=HALF)
                 w = turned[:].rearrange("p e (h t) j -> p e h t j", t=2)
                 nc.vector.tensor_tensor(
                     out=w[:, :, :, 0, :], in0=y[:, :, :, 1, :], in1=minus_sin[:].unsqueeze(2).to_broadcast(half), op=ALU.mult
@@ -242,7 +247,7 @@ def tile_llamaattention_pa_kernel(tc, hidden_states, Wq, Wk, Wv, out_0, out_1, o
                 if u >= 2:
                     m, pair = units[u - 2]
                     finish(m, pair, sums_of[u - 2])
-                sums_of[u] = multiply(codes, scales)
+                sums_of[u] = multiply(codes, scales, u >= n_units - SUM_BANKS)
             multiplied = ready
             if loaded == n_tiles:
                 for m, first_pair, count in to_store:

@@ -38,7 +38,8 @@ JOINED_FROM = 5
 TRANSPOSE_BANKS = 6
 SUM_BANKS = 2
 STORE_UNITS = 4
-SINGLE_RUNS = 4
+SINGLE_RUNS = 6
+EARLY = 2
 
 FLOPS = 2 * S * H * 3 * HEADS * HD
 
@@ -47,8 +48,9 @@ def tile_llamaattention_pa_kernel(tc, hidden_states, Wq, Wk, Wv, out_0, out_1, o
     nc = tc.nc
     weights = [Wq, Wk, Wv]
     outputs = [out_0, out_1, out_2]
-    units = [(m, first + d) for first in range(0, UNITS_PER_W, 2) for m in (0, 1) for d in (0, 1)]
-    units += [(2, pair) for pair in range(UNITS_PER_W)]
+    units = [(2, pair) for pair in range(EARLY)]
+    units += [(m, first + d) for first in range(0, UNITS_PER_W, 2) for m in (0, 1) for d in (0, 1)]
+    units += [(2, pair) for pair in range(EARLY, UNITS_PER_W)]
 
     with ExitStack() as ctx:
         ctx.enter_context(tc.manual_schedule())
@@ -101,38 +103,49 @@ def tile_llamaattention_pa_kernel(tc, hidden_states, Wq, Wk, Wv, out_0, out_1, o
                     out=codes[:, cols].bitcast(FP8X4), scales=scales[:, cols], in_=flat[:, 4 * cols.start : 4 * cols.stop]
                 )
 
+        def multiply_into(sums, e, codes, scales, first, width):
+            for g in range(PASSES):
+                x_cols = slice(g * ROWS + e * P, g * ROWS + (e + 1) * P)
+                w_cols = slice(g * ROWS + first, g * ROWS + first + width)
+                nc.tensor.matmul_mx(
+                    out=sums,
+                    lhsT=x_codes[:, x_cols].bitcast(FP8X4),
+                    lhsT_scale=x_scales[:, x_cols],
+                    rhs=codes[:, w_cols].bitcast(FP8X4),
+                    rhs_scale=scales[:, w_cols],
+                    start=(g == 0),
+                    stop=(g == PASSES - 1),
+                )
+
+        def transpose_bank():
+            bank = bank_pool.tile([P, 2, BLOCKS, P], F32, name="bank")
+            return bank[:]
+
         def multiply(codes, scales, in_transpose_bank):
             if in_transpose_bank:
-                bank = bank_pool.tile([P, 2, BLOCKS, P], F32, name="bank")
-                sums = bank[:].rearrange("p u b r -> p u (b r)")
+                sums = transpose_bank().rearrange("p u b r -> p u (b r)")
             else:
                 sum_bank = sum_pool.tile([P, 2, ROWS], F32, name="sum_bank")
                 sums = sum_bank[:]
             for e in range(2):
-                for g in range(PASSES):
-                    x_cols = slice(g * ROWS + e * P, g * ROWS + (e + 1) * P)
-                    w_cols = slice(g * ROWS, (g + 1) * ROWS)
-                    nc.tensor.matmul_mx(
-                        out=sums[:, e, :],
-                        lhsT=x_codes[:, x_cols].bitcast(FP8X4),
-                        lhsT_scale=x_scales[:, x_cols],
-                        rhs=codes[:, w_cols].bitcast(FP8X4),
-                        rhs_scale=scales[:, w_cols],
-                        start=(g == 0),
-                        stop=(g == PASSES - 1),
-                    )
+                multiply_into(sums[:, e, :], e, codes, scales, 0, ROWS)
             return sums
 
         shared = {}
         to_store = []
 
-        def finish(m, pair, sums):
+        def finish(m, pair, sums, on_scalar=False):
             group = (m, pair // STORE_UNITS)
             if group not in shared:
                 shared[group] = out_pool.tile([P, STORE_UNITS * UNIT_HEADS, 2, HD], F32, name="result")
             first_head = (pair % STORE_UNITS) * UNIT_HEADS
             result = shared[group][:, first_head : first_head + UNIT_HEADS]
-            if m == 2:
+            if m == 2 and on_scalar:
+                nc.scalar.copy(
+                    out=result.rearrange("p h e f -> p e h f"),
+                    in_=sums.rearrange("p e (h f) -> p e h f", f=HD),
+                )
+            elif m == 2:
                 nc.vector.tensor_copy(
                     out=result.rearrange("p h e f -> p e h f"),
                     in_=sums.rearrange("p e (h f) -> p e h f", f=HD),
@@ -163,17 +176,27 @@ def tile_llamaattention_pa_kernel(tc, hidden_states, Wq, Wk, Wv, out_0, out_1, o
                     op=ALU.add,
                 )
             if group == (2, UNITS_PER_W // STORE_UNITS - 1):
-                to_store.append((m, pair, 1))
+                to_store.append((m, pair * UNIT_HEADS, UNIT_HEADS))
             elif pair % STORE_UNITS == STORE_UNITS - 1:
-                to_store.append((m, pair - (STORE_UNITS - 1), STORE_UNITS))
+                to_store.append((m, (pair - (STORE_UNITS - 1)) * UNIT_HEADS, STORE_UNITS * UNIT_HEADS))
 
-        def store(m, first_pair, count):
-            heads = count * UNIT_HEADS
-            first_head = first_pair * UNIT_HEADS
-            in_tile = (first_pair % STORE_UNITS) * UNIT_HEADS
+        def finish_last(m, pair, codes, scales):
+            result = shared[(m, pair // STORE_UNITS)]
+            for h in range(UNIT_HEADS):
+                in_tile = (pair % STORE_UNITS) * UNIT_HEADS + h
+                quarters = [transpose_bank()[:, 0, 0, :] for e in range(2)]
+                for e in range(2):
+                    multiply_into(quarters[e], e, codes, scales, h * HD, HD)
+                nc.scalar.copy(out=result[:, in_tile, 0, :], in_=quarters[0])
+                nc.vector.tensor_copy(out=result[:, in_tile, 1, :], in_=quarters[1])
+                store(m, pair * UNIT_HEADS + h, 1)
+
+        def store(m, first_head, heads):
+            group_heads = STORE_UNITS * UNIT_HEADS
+            in_tile = first_head % group_heads
             nc.sync.dma_start(
                 out=outputs[m][0, first_head : first_head + heads].rearrange("h (p e) f -> p h (e f)", e=2),
-                in_=shared[(m, first_pair // STORE_UNITS)][:, in_tile : in_tile + heads].rearrange("p h e f -> p h (e f)"),
+                in_=shared[(m, first_head // group_heads)][:, in_tile : in_tile + heads].rearrange("p h e f -> p h (e f)"),
             )
 
         x_raw = consts.tile([P, BLOCKS, H], BF16, name="x_raw")
@@ -237,25 +260,26 @@ def tile_llamaattention_pa_kernel(tc, hidden_states, Wq, Wk, Wv, out_0, out_1, o
             if len(run) == 2:
                 ready = run[0]
             elif len(run) == 1:
-                ready = max(run[0] - 1, 0)
+                ready = max(run[0] - 1, min(run[0], EARLY))
             else:
                 ready = n_units
             for u in range(multiplied, ready):
                 codes = mx_pool.tile([P, PASSES * ROWS], U32, name="codes", align_bytes=64)
                 scales = mx_pool.tile([P, PASSES * ROWS], U8, name="scales", align_bytes=64)
-                quantise_rows(groupeds[u], codes, scales, PASSES if u == last else 1)
+                quantise_rows(groupeds[u], codes, scales, PASSES if u < EARLY or u == last else 1)
                 if u >= 2:
                     m, pair = units[u - 2]
-                    finish(m, pair, sums_of[u - 2])
-                sums_of[u] = multiply(codes, scales, u >= n_units - SUM_BANKS)
+                    finish(m, pair, sums_of[u - 2], on_scalar=(u == last))
+                if u < last:
+                    sums_of[u] = multiply(codes, scales, u == last - 1)
             multiplied = ready
             if loaded == n_tiles:
-                for m, first_pair, count in to_store:
-                    store(m, first_pair, count)
+                for m, first_head, heads in to_store:
+                    store(m, first_head, heads)
                 to_store.clear()
-        for u in range(n_units - 2, n_units):
-            m, pair = units[u]
-            finish(m, pair, sums_of[u])
-            for m, first_pair, count in to_store:
-                store(m, first_pair, count)
-            to_store.clear()
+        m, pair = units[last - 1]
+        finish(m, pair, sums_of[last - 1], on_scalar=True)
+        for m, first_head, heads in to_store:
+            store(m, first_head, heads)
+        m, pair = units[last]
+        finish_last(m, pair, codes, scales)

@@ -33,6 +33,7 @@ UNITS_PER_W = HEADS // UNIT_HEADS
 
 ROUND_MAGIC = 1.5 * 2.0**23
 
+DMA_ALIGN = 256
 RAW_BUFS = 5
 JOINED_FROM = 5
 TRANSPOSE_BANKS = 6
@@ -66,7 +67,7 @@ def tile_llamaattention_pa_kernel(tc, hidden_states, Wq, Wk, Wv, out_0, out_1, o
         def load_tile(t):
             m, pair = units[2 * t]
             rows = weights[m][pair * ROWS : (pair + 2) * ROWS, :].rearrange("(c p) k -> p c k", p=P)
-            raw = raw_pool.tile([P, 2 * BLOCKS, H], BF16, name="raw")
+            raw = raw_pool.tile([P, 2 * BLOCKS, H], BF16, name="raw", align_bytes=DMA_ALIGN)
             if t >= JOINED_FROM:
                 nc.sync.dma_start(out=raw[:], in_=rows)
             else:
@@ -137,7 +138,7 @@ def tile_llamaattention_pa_kernel(tc, hidden_states, Wq, Wk, Wv, out_0, out_1, o
         def finish(m, pair, sums, on_scalar=False):
             group = (m, pair // STORE_UNITS)
             if group not in shared:
-                shared[group] = out_pool.tile([P, STORE_UNITS * UNIT_HEADS, 2, HD], F32, name="result")
+                shared[group] = out_pool.tile([P, STORE_UNITS * UNIT_HEADS, 2, HD], F32, name="result", align_bytes=DMA_ALIGN)
             first_head = (pair % STORE_UNITS) * UNIT_HEADS
             result = shared[group][:, first_head : first_head + UNIT_HEADS]
             if m == 2 and on_scalar:
@@ -199,7 +200,7 @@ def tile_llamaattention_pa_kernel(tc, hidden_states, Wq, Wk, Wv, out_0, out_1, o
                 in_=shared[(m, first_head // group_heads)][:, in_tile : in_tile + heads].rearrange("p h e f -> p h (e f)"),
             )
 
-        x_raw = consts.tile([P, BLOCKS, H], BF16, name="x_raw")
+        x_raw = consts.tile([P, BLOCKS, H], BF16, name="x_raw", align_bytes=DMA_ALIGN)
         nc.sync.dma_start(out=x_raw[:], in_=hidden_states[0].rearrange("(p e) k -> p e k", e=2))
         raws = {}
         for t in range(RAW_BUFS):

@@ -66,14 +66,14 @@ def tile_llamaattention_pa_kernel(tc, hidden_states, Wq, Wk, Wv, out_0, out_1, o
 
         def load_tile(t):
             m, pair = units[2 * t]
-            rows = weights[m][pair * ROWS : (pair + 2) * ROWS, :].rearrange("(c p) k -> p c k", p=P)
+            rows = weights[m][pair * ROWS : (pair + 2) * ROWS, :].rearrange("(d p c) k -> p d c k", p=P, c=BLOCKS)
             raw = raw_pool.tile([P, 2 * BLOCKS, H], BF16, name="raw", align_bytes=DMA_ALIGN)
             if t >= JOINED_FROM:
-                nc.sync.dma_start(out=raw[:], in_=rows)
+                nc.sync.dma_start(out=raw[:].rearrange("p (d c) k -> p d c k", c=BLOCKS), in_=rows)
             else:
                 for d in range(2):
                     blocks = slice(d * BLOCKS, (d + 1) * BLOCKS)
-                    nc.sync.dma_start(out=raw[:, blocks, :], in_=rows[:, blocks, :])
+                    nc.sync.dma_start(out=raw[:, blocks, :], in_=rows[:, d])
             for d in range(2):
                 raws[2 * t + d] = raw[:, d * BLOCKS : (d + 1) * BLOCKS, :]
 
@@ -254,7 +254,7 @@ def tile_llamaattention_pa_kernel(tc, hidden_states, Wq, Wk, Wv, out_0, out_1, o
         multiplied = 0
         for run in runs:
             for u in run:
-                groupeds[u] = transpose_rows(raws[u], "b r")
+                groupeds[u] = transpose_rows(raws[u], "r b")
                 if u % 2 == 1 and loaded < n_tiles:
                     load_tile(loaded)
                     loaded += 1

import math
from contextlib import ExitStack

import concourse.mybir as mybir
from concourse.masks import make_identity

F32 = mybir.dt.float32
BF16 = mybir.dt.bfloat16
I32 = mybir.dt.int32
U32 = mybir.dt.uint32
U8 = mybir.dt.uint8
FP8X4 = mybir.dt.float8_e4m3fn_x4
ALU = mybir.AluOpType
ACT = mybir.ActivationFunctionType

P = 128
S = 256
H = 2048
HEADS = 16
HD = 128
HALF = HD // 2
ROPE_BASE = 10000.0
DOUBLINGS = 6
assert 2**DOUBLINGS == HALF

K_PASS = 512
PASSES = H // K_PASS
WORDS_PASS = K_PASS // 2
ROWS = 256
BLOCKS = ROWS // P
UNIT_HEADS = ROWS // HD
UNITS_PER_W = HEADS // UNIT_HEADS

ROUND_MAGIC = 1.5 * 2.0**23

DMA_ALIGN = 256
RAW_BUFS = 5
JOINED_FROM = 5
TRANSPOSE_BANKS = 6
SUM_BANKS = 2
STORE_UNITS = 4
SINGLE_RUNS = 6
EARLY = 2

FLOPS = 2 * S * H * 3 * HEADS * HD


def tile_llamaattention_pa_kernel(tc, hidden_states, Wq, Wk, Wv, out_0, out_1, out_2):
    nc = tc.nc
    weights = [Wq, Wk, Wv]
    outputs = [out_0, out_1, out_2]
    units = [(2, pair) for pair in range(EARLY)]
    units += [(m, first + d) for first in range(0, UNITS_PER_W, 2) for m in (0, 1) for d in (0, 1)]
    units += [(2, pair) for pair in range(EARLY, UNITS_PER_W)]

    with ExitStack() as ctx:
        ctx.enter_context(tc.manual_schedule())
        consts = ctx.enter_context(tc.tile_pool(name="consts", bufs=1))
        raw_pool = ctx.enter_context(tc.tile_pool(name="raw", bufs=RAW_BUFS))
        grouped_pool = ctx.enter_context(tc.tile_pool(name="grouped", bufs=5))
        mx_pool = ctx.enter_context(tc.tile_pool(name="mx", bufs=5))
        work = ctx.enter_context(tc.tile_pool(name="work", bufs=3))
        out_pool = ctx.enter_context(tc.tile_pool(name="out", bufs=len(units) // STORE_UNITS))
        bank_pool = ctx.enter_context(tc.psum_pool(name="banks", bufs=TRANSPOSE_BANKS))
        sum_pool = ctx.enter_context(tc.psum_pool(name="sums", bufs=SUM_BANKS))

        def load_tile(t):
            m, pair = units[2 * t]
            rows = weights[m][pair * ROWS : (pair + 2) * ROWS, :].rearrange("(d p c) k -> p d c k", p=P, c=BLOCKS)
            raw = raw_pool.tile([P, 2 * BLOCKS, H], BF16, name="raw", align_bytes=DMA_ALIGN)
            if t >= JOINED_FROM:
                nc.sync.dma_start(out=raw[:].rearrange("p (d c) k -> p d c k", c=BLOCKS), in_=rows)
            else:
                for d in range(2):
                    blocks = slice(d * BLOCKS, (d + 1) * BLOCKS)
                    nc.sync.dma_start(out=raw[:, blocks, :], in_=rows[:, d])
            for d in range(2):
                raws[2 * t + d] = raw[:, d * BLOCKS : (d + 1) * BLOCKS, :]

        def transpose_rows(raw, column_order):
            raw_words = raw.bitcast(F32)
            grouped = grouped_pool.tile([P, PASSES, ROWS * 4], BF16, name="grouped", align_bytes=64)
            grouped_words = grouped[:].bitcast(F32)
            for g in range(PASSES):
                bank = bank_pool.tile([P, 2, BLOCKS, P], F32, name="bank")
                for u in range(2):
                    first = g * WORDS_PASS + u * P
                    for b in range(BLOCKS):
                        nc.tensor.transpose(
                            out=bank[:, u, b, :], in_=raw_words[:, b, first : first + P], identity=ident[:]
                        )
                nc.scalar.copy(
                    out=grouped_words[:, g].rearrange("p (%s u) -> p %s u" % (column_order, column_order), b=BLOCKS, u=2),
                    in_=bank[:].rearrange("p u b r -> p %s u" % column_order),
                )
            return grouped

        def quantise_rows(grouped, codes, scales, calls=1):
            flat = grouped[:].rearrange("p g c -> p (g c)")
            width = PASSES * ROWS // calls
            for call in range(calls):
                cols = slice(call * width, (call + 1) * width)
                nc.vector.quantize_mx(
                    out=codes[:, cols].bitcast(FP8X4), scales=scales[:, cols], in_=flat[:, 4 * cols.start : 4 * cols.stop]
                )

        def multiply_into(sums, e, codes, scales, first, width):
            for g in range(PASSES):
                x_cols = slice(g * ROWS + e * P, g * ROWS + (e + 1) * P)
                w_cols = slice(g * ROWS + first, g * ROWS + first + width)
                nc.tensor.matmul_mx(
                    out=sums,
                    lhsT=x_codes[:, x_cols].bitcast(FP8X4),
                    lhsT_scale=x_scales[:, x_cols],
                    rhs=codes[:, w_cols].bitcast(FP8X4),
                    rhs_scale=scales[:, w_cols],
                    start=(g == 0),
                    stop=(g == PASSES - 1),
                )

        def transpose_bank():
            bank = bank_pool.tile([P, 2, BLOCKS, P], F32, name="bank")
            return bank[:]

        def multiply(codes, scales, in_transpose_bank):
            if in_transpose_bank:
                sums = transpose_bank().rearrange("p u b r -> p u (b r)")
            else:
                sum_bank = sum_pool.tile([P, 2, ROWS], F32, name="sum_bank")
                sums = sum_bank[:]
            for e in range(2):
                multiply_into(sums[:, e, :], e, codes, scales, 0, ROWS)
            return sums

        shared = {}
        to_store = []

        def finish(m, pair, sums, on_scalar=False):
            group = (m, pair // STORE_UNITS)
            if group not in shared:
                shared[group] = out_pool.tile([P, STORE_UNITS * UNIT_HEADS, 2, HD], F32, name="result", align_bytes=DMA_ALIGN)
            first_head = (pair % STORE_UNITS) * UNIT_HEADS
            result = shared[group][:, first_head : first_head + UNIT_HEADS]
            if m == 2 and on_scalar:
                nc.scalar.copy(
                    out=result.rearrange("p h e f -> p e h f"),
                    in_=sums.rearrange("p e (h f) -> p e h f", f=HD),
                )
            elif m == 2:
                nc.vector.tensor_copy(
                    out=result.rearrange("p h e f -> p e h f"),
                    in_=sums.rearrange("p e (h f) -> p e h f", f=HD),
                )
            else:
                halves = [P, 2, UNIT_HEADS * 2, HALF]
                half = [P, 2, UNIT_HEADS, HALF]
                by_cos = work.tile(halves, F32, name="by_cos")
                turned = work.tile(halves, F32, name="turned")
                nc.vector.tensor_tensor(
                    out=by_cos[:],
                    in0=sums.rearrange("p e (c j) -> p e c j", j=HALF),
                    in1=cos_sin[:, :, 0, :].unsqueeze(2).to_broadcast(halves),
                    op=ALU.mult,
                )
                y = sums.rearrange("p e (h t j) -> p e h t j", t=2, j=HALF)
                w = turned[:].rearrange("p e (h t) j -> p e h t j", t=2)
                nc.vector.tensor_tensor(
                    out=w[:, :, :, 0, :], in0=y[:, :, :, 1, :], in1=minus_sin[:].unsqueeze(2).to_broadcast(half), op=ALU.mult
                )
                nc.vector.tensor_tensor(
                    out=w[:, :, :, 1, :], in0=y[:, :, :, 0, :], in1=cos_sin[:, :, 1, :].unsqueeze(2).to_broadcast(half), op=ALU.mult
                )
                nc.gpsimd.tensor_tensor(
                    out=result.rearrange("p h e f -> p e h f"),
                    in0=by_cos[:].rearrange("p e (h t) j -> p e h (t j)", t=2),
                    in1=turned[:].rearrange("p e (h t) j -> p e h (t j)", t=2),
                    op=ALU.add,
                )
            if group == (2, UNITS_PER_W // STORE_UNITS - 1):
                to_store.append((m, pair * UNIT_HEADS, UNIT_HEADS))
            elif pair % STORE_UNITS == STORE_UNITS - 1:
                to_store.append((m, (pair - (STORE_UNITS - 1)) * UNIT_HEADS, STORE_UNITS * UNIT_HEADS))

        def finish_last(m, pair, codes, scales):
            result = shared[(m, pair // STORE_UNITS)]
            for h in range(UNIT_HEADS):
                in_tile = (pair % STORE_UNITS) * UNIT_HEADS + h
                quarters = [transpose_bank()[:, 0, 0, :] for e in range(2)]
                for e in range(2):
                    multiply_into(quarters[e], e, codes, scales, h * HD, HD)
                nc.scalar.copy(out=result[:, in_tile, 0, :], in_=quarters[0])
                nc.vector.tensor_copy(out=result[:, in_tile, 1, :], in_=quarters[1])
                store(m, pair * UNIT_HEADS + h, 1)

        def store(m, first_head, heads):
            group_heads = STORE_UNITS * UNIT_HEADS
            in_tile = first_head % group_heads
            nc.sync.dma_start(
                out=outputs[m][0, first_head : first_head + heads].rearrange("h (p e) f -> p h (e f)", e=2),
                in_=shared[(m, first_head // group_heads)][:, in_tile : in_tile + heads].rearrange("p h e f -> p h (e f)"),
            )

        x_raw = consts.tile([P, BLOCKS, H], BF16, name="x_raw", align_bytes=DMA_ALIGN)
        nc.sync.dma_start(out=x_raw[:], in_=hidden_states[0].rearrange("(p e) k -> p e k", e=2))
        raws = {}
        for t in range(RAW_BUFS):
            load_tile(t)

        ident = consts.tile([P, P], F32, name="ident")
        make_identity(nc, ident[:])
        position_int = consts.tile([P, 2], I32, name="position_int")
        nc.gpsimd.iota(position_int[:], pattern=[[1, 2]], base=0, channel_multiplier=2)
        position_turns = consts.tile([P, 2], F32, name="position_turns")
        nc.vector.tensor_scalar_mul(out=position_turns[:], in0=position_int[:], scalar1=1.0 / (2.0 * math.pi))

        inv_freq = consts.tile([P, HALF], F32, name="inv_freq")
        nc.vector.memset(inv_freq[:, 0:1], 1.0)
        for doubling in range(DOUBLINGS):
            width = 2**doubling
            nc.vector.tensor_scalar_mul(
                out=inv_freq[:, width : 2 * width],
                in0=inv_freq[:, 0:width],
                scalar1=ROPE_BASE ** (-width / HALF),
            )

        turns = consts.tile([P, 2, 2, HALF], F32, name="turns")
        for e in range(2):
            nc.vector.tensor_scalar(
                out=turns[:, e, 0, :], in0=inv_freq[:], scalar1=position_turns[:, e : e + 1], scalar2=0.25,
                op0=ALU.mult, op1=ALU.add,
            )
            nc.vector.tensor_scalar_mul(out=turns[:, e, 1, :], in0=inv_freq[:], scalar1=position_turns[:, e : e + 1])
        whole_turns = consts.tile([P, 2, 2, HALF], F32, name="whole_turns")
        nc.vector.tensor_scalar(
            out=whole_turns[:], in0=turns[:], scalar1=ROUND_MAGIC, scalar2=ROUND_MAGIC, op0=ALU.add, op1=ALU.subtract
        )
        part_turns = consts.tile([P, 2, 2, HALF], F32, name="part_turns")
        nc.vector.tensor_tensor(out=part_turns[:], in0=turns[:], in1=whole_turns[:], op=ALU.subtract)
        cos_sin = consts.tile([P, 2, 2, HALF], F32, name="cos_sin")
        nc.scalar.activation(out=cos_sin[:], in_=part_turns[:], func=ACT.Sin, scale=2.0 * math.pi)
        minus_sin = consts.tile([P, 2, HALF], F32, name="minus_sin")
        nc.vector.tensor_scalar_mul(out=minus_sin[:], in0=cos_sin[:, :, 1, :], scalar1=-1.0)

        x_codes = consts.tile([P, PASSES * ROWS], U32, name="x_codes", align_bytes=64)
        x_scales = consts.tile([P, PASSES * ROWS], U8, name="x_scales", align_bytes=64)
        quantise_rows(transpose_rows(x_raw[:], "b r"), x_codes, x_scales)

        n_units = len(units)
        last = n_units - 1
        runs = [[u] for u in range(SINGLE_RUNS)] + [[u, u + 1] for u in range(SINGLE_RUNS, n_units, 2)] + [[]]
        groupeds, sums_of = {}, {}
        n_tiles = n_units // 2
        loaded = RAW_BUFS
        multiplied = 0
        for run in runs:
            for u in run:
                groupeds[u] = transpose_rows(raws[u], "r b")
                if u % 2 == 1 and loaded < n_tiles:
                    load_tile(loaded)
                    loaded += 1
            if len(run) == 2:
                ready = run[0]
            elif len(run) == 1:
                ready = max(run[0] - 1, min(run[0], EARLY))
            else:
                ready = n_units
            for u in range(multiplied, ready):
                codes = mx_pool.tile([P, PASSES * ROWS], U32, name="codes", align_bytes=64)
                scales = mx_pool.tile([P, PASSES * ROWS], U8, name="scales", align_bytes=64)
                quantise_rows(groupeds[u], codes, scales, PASSES if u < EARLY or u == last else 1)
                if u >= 2:
                    m, pair = units[u - 2]
                    finish(m, pair, sums_of[u - 2], on_scalar=(u == last))
                if u < last:
                    sums_of[u] = multiply(codes, scales, u == last - 1)
            multiplied = ready
            if loaded == n_tiles:
                for m, first_head, heads in to_store:
                    store(m, first_head, heads)
                to_store.clear()
        m, pair = units[last - 1]
        finish(m, pair, sums_of[last - 1], on_scalar=True)
        for m, first_head, heads in to_store:
            store(m, first_head, heads)
        m, pair = units[last]
        finish_last(m, pair, codes, scales)
